import numpy as np
import ml_dtypes


def mxq(x, axis, fmt="e4m3"):
    dtype, down = {"e4m3": (ml_dtypes.float8_e4m3fn, 7), "e5m2": (ml_dtypes.float8_e5m2, 14)}[fmt]
    v = np.moveaxis(np.asarray(x, np.float32).astype(ml_dtypes.bfloat16).astype(np.float64), axis, -1)
    blocks = v.reshape(v.shape[:-1] + (-1, 32))
    amax = np.abs(blocks).max(-1, keepdims=True)
    byte = np.maximum(np.where(amax > 0, np.frexp(amax)[1] - 1 + 127, 0) - down, 1)
    scale = np.exp2(byte - 127.0)
    codes = (blocks / scale).astype(np.float32).astype(dtype).astype(np.float64)
    return np.moveaxis((codes * scale).reshape(v.shape), -1, axis)


WIDE = False


def mx_kscale(k):
    if not WIDE:
        return np.ones(k)
    levels = np.array([10, -10, 5, -5, 0])
    a = np.random.permutation(np.resize(levels, k // 512 * 4)).reshape(k // 512, 4)
    idx = np.arange(k)
    return np.exp2(a[idx // 512, idx % 128 // 32])


BF16 = ml_dtypes.bfloat16


def bf(x):
    return np.asarray(x, np.float32).astype(BF16)


def f64(x):
    return np.asarray(x).astype(np.float64)


N, C, E, T, H, CK = 3, 512, 256, 4096, 8, 64
EPS = 1e-5


def setup_inputs():
    s = mx_kscale(C)
    return {
        "h_attn": bf(np.random.standard_normal((N, T, C)) * 0.4 * s),
        "x": bf(np.random.standard_normal((N, E, T))),
        "masks": bf(np.random.uniform(0.2, 1.0, (N, 1, T))),
        "Wo": bf(np.random.standard_normal((E, C)) * 2.0 / np.sqrt(C) / s[None, :]),
        "bo": bf(np.random.standard_normal(E) * 0.5),
    }


def reference(h_attn, x, masks, Wo, bo):
    o = (mxq(f64(h_attn), 2, "e4m3") @ mxq(f64(Wo), 1, "e4m3").T) + f64(bo)
    y = o.transpose(0, 2, 1) * f64(masks) + f64(x)
    mean = y.mean(-1, keepdims=True)
    var = np.square(y - mean).mean(-1, keepdims=True)
    return (y - mean) / np.sqrt(var + EPS)

@@ -1,0 +1,299 @@
+from contextlib import ExitStack
+
+import concourse.mybir as mybir
+from concourse.masks import make_identity
+
+F32 = mybir.dt.float32
+BF16 = mybir.dt.bfloat16
+U32 = mybir.dt.uint32
+U8 = mybir.dt.uint8
+FP8X4 = mybir.dt.float8_e4m3fn_x4
+ALU = mybir.AluOpType
+ACT = mybir.ActivationFunctionType
+
+P = 128
+SEQS, FRAMES, C_IN, C_OUT = 3, 4096, 512, 256
+EPS = 1e-5
+ROOT_SCALE = FRAMES**-0.5
+FLOPS = 2 * SEQS * FRAMES * C_IN * C_OUT
+
+WORDS = C_IN // 2
+BLOCK = 512
+ROWS = BLOCK // P
+BLOCKS_PER_SEQ = FRAMES // BLOCK
+BLOCKS = SEQS * BLOCKS_PER_SEQ
+STEP = 2 * BLOCK
+STEPS_PER_GROUP = FRAMES // STEP
+GROUPS = SEQS * (C_OUT // P)
+STEPS = GROUPS * STEPS_PER_GROUP
+STEPS_PER_SEQ = STEPS // SEQS
+
+LOAD_AHEAD = 16
+FLIP_AHEAD = 8
+QUANTISE_AHEAD = FLIP_AHEAD - 1
+MULTIPLY_AHEAD = 1
+SQUARES_BEHIND = 1
+NORM_BEHIND = STEPS_PER_GROUP + 1
+SPREAD_AHEAD = 6
+RESIDUAL_AHEAD = 9
+
+NORM_VECTOR_COLS = STEP // 2
+
+
+def tile_transformerencoderblock_pa_t_kernel(tc, h_attn, x, masks, Wo, bo, out):
+    nc = tc.nc
+    with ExitStack() as ctx:
+        const = ctx.enter_context(tc.tile_pool(name="const", bufs=1))
+        frames_in = ctx.enter_context(tc.tile_pool(name="frames_in", bufs=LOAD_AHEAD - FLIP_AHEAD))
+        stage = ctx.enter_context(tc.tile_pool(name="stage", bufs=3))
+        per_seq = ctx.enter_context(tc.tile_pool(name="per_seq", bufs=2))
+        per_group = ctx.enter_context(tc.tile_pool(name="per_group", bufs=3))
+        psum = ctx.enter_context(tc.psum_pool(name="psum", bufs=1))
+        ctx.enter_context(tc.manual_schedule())
+
+        ident_f32 = const.tile([P, P], F32)
+        make_identity(nc, ident_f32[:])
+        ident_bf16 = const.tile([P, P], BF16)
+        make_identity(nc, ident_bf16[:])
+        minus_half = const.tile([P, 1], F32)
+        nc.gpsimd.memset(minus_half[:], -0.5)
+
+        raw, grouped = {}, {}
+        codes, scales, mask_rows = {}, {}, {}
+        product = {}
+        residual, y, sums, pivot, neg_mean, base, rstd, shift = {}, {}, {}, {}, {}, {}, {}, {}
+
+        def flip_two(rows_words, grouped_words, by_vector):
+            bank = psum.tile([P, 2, 2, P], F32, tag="flip", bufs=3)
+            for row_block in range(2):
+                for half_row in range(2):
+                    first = WORDS * row_block + P * half_row
+                    nc.tensor.transpose(
+                        bank[:, row_block, half_row, :], rows_words[:, first : first + P], ident_f32[:]
+                    )
+            dst = grouped_words.rearrange("w (b r u) -> w b r u", b=2, u=2)
+            src = bank[:].rearrange("w b u r -> w b r u")
+            if by_vector:
+                nc.vector.tensor_copy(out=dst, in_=src)
+            else:
+                nc.scalar.copy(out=dst, in_=src)
+
+        small_rows = const.tile([P, P], BF16)
+        nc.vector.memset(small_rows[:], 0.0)
+        mask_row_count = SEQS * FRAMES // P
+        nc.scalar.dma_start(
+            out=small_rows[0:mask_row_count, :], in_=masks.rearrange("n o (i r) -> (n o i) r", r=P)
+        )
+        nc.scalar.dma_start(
+            out=small_rows[mask_row_count : mask_row_count + C_OUT // P, :],
+            in_=bo.rearrange("(h r) -> h r", r=P),
+        )
+        w_raw = const.tile([P, 2 * C_IN], BF16)
+        nc.scalar.dma_start(
+            out=w_raw[:].rearrange("p (h k) -> p h k", h=2), in_=Wo.rearrange("(h p) k -> p h k", p=P)
+        )
+
+        def prepare_small_inputs():
+            small_cols = psum.tile([P, BLOCK], BF16, tag="spread", bufs=1)
+            nc.tensor.transpose(small_cols[:, 0:P], small_rows[:], ident_bf16[:])
+            nc.vector.tensor_copy(out=mask_cols[:], in_=small_cols[:, 0:mask_row_count])
+            nc.vector.tensor_copy(
+                out=bias_cols[:], in_=small_cols[:, mask_row_count : mask_row_count + C_OUT // P]
+            )
+            flip_two(w_raw[:].bitcast(F32), w_grouped[:].bitcast(F32), True)
+            nc.vector.quantize_mx(out=w_codes[:].bitcast(FP8X4), scales=w_scales[:], in_=w_grouped[:])
+
+        mask_cols = const.tile([P, mask_row_count], BF16)
+        bias_cols = const.tile([P, C_OUT // P], F32)
+        w_grouped = const.tile([P, 2 * C_IN], BF16, align_bytes=64)
+        w_codes = const.tile([P, C_OUT], U32, align_bytes=64)
+        w_scales = const.tile([P, C_OUT], U8, align_bytes=64)
+
+        def load_block(block):
+            seq, b = divmod(block, BLOCKS_PER_SEQ)
+            raw[block] = frames_in.tile([P, ROWS * C_IN], BF16, name="raw")
+            nc.sync.dma_start(
+                out=raw[block][:],
+                in_=h_attn[seq, BLOCK * b : BLOCK * (b + 1), :].rearrange("(p a) k -> p (a k)", a=ROWS),
+            )
+
+        def load_residual(group):
+            seq, half = divmod(group, C_OUT // P)
+            residual[group] = per_group.tile([P, FRAMES], BF16, name="residual")
+            nc.sync.dma_start(out=residual[group][:], in_=x[seq, P * half : P * (half + 1), :])
+
+        def flip_block(block):
+            seq, b = divmod(block, BLOCKS_PER_SEQ)
+            if b == 0:
+                codes[seq] = per_seq.tile([P, FRAMES], U32, name="codes", align_bytes=64)
+                scales[seq] = per_seq.tile([P, FRAMES], U8, name="scales", align_bytes=64)
+            grouped[block] = stage.tile([P, 4 * BLOCK], BF16, name="grouped", align_bytes=64)
+            raw_words = raw[block][:].bitcast(F32)
+            grouped_words = grouped[block][:].bitcast(F32)
+            for pair in range(ROWS // 2):
+                cols = slice(2 * WORDS * pair, 2 * WORDS * (pair + 1))
+                flip_two(raw_words[:, cols], grouped_words[:, cols], seq == 0 and pair == 1)
+
+        def spread_mask(block):
+            seq, b = divmod(block, BLOCKS_PER_SEQ)
+            if b == 0:
+                mask_rows[seq] = per_seq.tile([P, FRAMES], BF16, name="mask_rows")
+            spread = psum.tile([P, BLOCK], BF16, tag="spread", bufs=1)
+            for i in range(BLOCK // P):
+                col = (FRAMES // P) * seq + (BLOCK // P) * b + i
+                nc.tensor.transpose(
+                    spread[:, P * i : P * (i + 1)],
+                    mask_cols[:, col : col + 1].to_broadcast([P, P]),
+                    ident_bf16[:],
+                )
+            nc.scalar.copy(out=mask_rows[seq][:, BLOCK * b : BLOCK * (b + 1)], in_=spread[:])
+
+        def quantise_block(block):
+            seq, b = divmod(block, BLOCKS_PER_SEQ)
+            cols = slice(BLOCK * b, BLOCK * (b + 1))
+            nc.vector.quantize_mx(
+                out=codes[seq][:, cols].bitcast(FP8X4), scales=scales[seq][:, cols], in_=grouped[block][:]
+            )
+
+        def where(step):
+            group, j = divmod(step, STEPS_PER_GROUP)
+            seq, half = divmod(group, C_OUT // P)
+            return seq, half, group, j
+
+        def multiply(step):
+            seq, half, group, j = where(step)
+            for i in range(STEP // BLOCK):
+                cols = slice(STEP * j + BLOCK * i, STEP * j + BLOCK * (i + 1))
+                product[(step, i)] = psum.tile([P, BLOCK], F32, tag="product", bufs=4, name="product")
+                nc.tensor.matmul_mx(
+                    out=product[(step, i)][:],
+                    lhsT=w_codes[:, P * half : P * (half + 1)].bitcast(FP8X4),
+                    lhsT_scale=w_scales[:, P * half : P * (half + 1)],
+                    rhs=codes[seq][:, cols].bitcast(FP8X4),
+                    rhs_scale=scales[seq][:, cols],
+                    start=True,
+                    stop=True,
+                )
+
+        def add_bias_and_mask(step):
+            seq, half, group, j = where(step)
+            if j == 0:
+                y[group] = per_group.tile([P, FRAMES], F32, name="y")
+                sums[group] = per_group.tile([P, 2, 8], F32, name="sums")
+            for i in range(STEP // BLOCK):
+                cols = slice(STEP * j + BLOCK * i, STEP * j + BLOCK * (i + 1))
+                nc.vector.scalar_tensor_tensor(
+                    out=y[group][:, cols].rearrange("e (p a) -> e p a", a=ROWS),
+                    in0=product[(step, i)][:].rearrange("e (a p) -> e p a", a=ROWS),
+                    scalar=bias_cols[:, half : half + 1],
+                    in1=mask_rows[seq][:, cols].rearrange("e (p a) -> e p a", a=ROWS),
+                    op0=ALU.add,
+                    op1=ALU.mult,
+                )
+
+        def add_residual(step):
+            seq, half, group, j = where(step)
+            cols = slice(STEP * j, STEP * (j + 1))
+            nc.vector.scalar_tensor_tensor(
+                out=y[group][:, cols],
+                in0=y[group][:, cols],
+                scalar=1.0,
+                in1=residual[group][:, cols],
+                op0=ALU.mult,
+                op1=ALU.add,
+                accum_out=sums[group][:, 0, j : j + 1],
+            )
+            if j == 0:
+                pivot[group] = per_group.tile([P, 2], F32, name="pivot")
+                for col, factor in enumerate((-1.0 / STEP, -ROOT_SCALE / STEP)):
+                    nc.gpsimd.tensor_scalar(
+                        out=pivot[group][:, col : col + 1], in0=sums[group][:, 0, 0:1],
+                        scalar1=factor, scalar2=0.0, op0=ALU.mult, op1=ALU.add,
+                    )
+
+        def sum_squares(step):
+            seq, half, group, j = where(step)
+            cols = slice(STEP * j, STEP * (j + 1))
+            squares = stage.tile([P, STEP], BF16, name="squares")
+            nc.scalar.activation(
+                out=squares[:], in_=y[group][:, cols], func=ACT.Square,
+                bias=pivot[group][:, 1:2], scale=ROOT_SCALE, accum_out=sums[group][:, 1, j : j + 1],
+            )
+
+        def add_columns(total, row, count):
+            nc.gpsimd.tensor_tensor(out=total, in0=row[:, 0:1], in1=row[:, 1:2], op=ALU.add)
+            for col in range(2, count):
+                nc.gpsimd.tensor_tensor(out=total, in0=total, in1=row[:, col : col + 1], op=ALU.add)
+
+        def early_statistics(group):
+            total = per_group.tile([P, 1], F32, name="total")
+            add_columns(total[:], sums[group][:, 0, :], STEPS_PER_GROUP)
+            neg_mean[group] = per_group.tile([P, 1], F32, name="neg_mean")
+            nc.gpsimd.tensor_scalar(
+                out=neg_mean[group][:], in0=total[:],
+                scalar1=-1.0 / FRAMES, scalar2=0.0, op0=ALU.mult, op1=ALU.add,
+            )
+            off = per_group.tile([P, 1], F32, name="off")
+            nc.gpsimd.tensor_tensor(out=off[:], in0=neg_mean[group][:], in1=pivot[group][:, 0:1], op=ALU.subtract)
+            off_sq = per_group.tile([P, 1], F32, name="off_sq")
+            nc.gpsimd.tensor_tensor(out=off_sq[:], in0=off[:], in1=off[:], op=ALU.mult)
+            rest = per_group.tile([P, 1], F32, name="rest")
+            nc.gpsimd.tensor_scalar(
+                out=rest[:], in0=off_sq[:], scalar1=-1.0, scalar2=EPS, op0=ALU.mult, op1=ALU.add
+            )
+            first_squares = per_group.tile([P, 1], F32, name="first_squares")
+            add_columns(first_squares[:], sums[group][:, 1, :], STEPS_PER_GROUP - 1)
+            base[group] = per_group.tile([P, 1], F32, name="base")
+            nc.gpsimd.tensor_tensor(out=base[group][:], in0=first_squares[:], in1=rest[:], op=ALU.add)
+
+        def late_statistics(group):
+            var_eps = per_group.tile([P, 1], F32, name="var_eps")
+            nc.gpsimd.tensor_tensor(
+                out=var_eps[:], in0=base[group][:],
+                in1=sums[group][:, 1, STEPS_PER_GROUP - 1 : STEPS_PER_GROUP], op=ALU.add,
+            )
+            rstd[group] = per_group.tile([P, 1], F32, name="rstd")
+            nc.gpsimd.tensor_tensor(out=rstd[group][:], in0=var_eps[:], in1=minus_half[:], op=ALU.pow)
+            shift[group] = per_group.tile([P, 1], F32, name="shift")
+            nc.gpsimd.tensor_tensor(out=shift[group][:], in0=neg_mean[group][:], in1=rstd[group][:], op=ALU.mult)
+
+        def normalise_and_store(step):
+            seq, half, group, j = where(step)
+            first, split, last = STEP * j, STEP * j + NORM_VECTOR_COLS, STEP * (j + 1)
+            nc.vector.tensor_scalar(
+                out=y[group][:, first:split], in0=y[group][:, first:split],
+                scalar1=rstd[group][:, 0:1], scalar2=shift[group][:, 0:1], op0=ALU.mult, op1=ALU.add,
+            )
+            nc.scalar.activation(
+                out=y[group][:, split:last], in_=y[group][:, split:last], func=ACT.Identity,
+                bias=shift[group][:, 0:1], scale=rstd[group][:, 0:1],
+            )
+            nc.sync.dma_start(out=out[seq, P * half : P * (half + 1), first:last], in_=y[group][:, first:last])
+
+        for r in range(-LOAD_AHEAD, STEPS + NORM_BEHIND):
+            if 0 <= r + MULTIPLY_AHEAD < STEPS:
+                multiply(r + MULTIPLY_AHEAD)
+            if 0 <= r + FLIP_AHEAD < BLOCKS:
+                flip_block(r + FLIP_AHEAD)
+            if r == -SPREAD_AHEAD:
+                prepare_small_inputs()
+            if 0 <= r + SPREAD_AHEAD < BLOCKS:
+                spread_mask(r + SPREAD_AHEAD)
+            if 0 <= r + LOAD_AHEAD < BLOCKS:
+                load_block(r + LOAD_AHEAD)
+            if 0 <= r - SQUARES_BEHIND < STEPS:
+                sum_squares(r - SQUARES_BEHIND)
+                if (r - SQUARES_BEHIND) % STEPS_PER_GROUP == STEPS_PER_GROUP - 1:
+                    late_statistics((r - SQUARES_BEHIND) // STEPS_PER_GROUP)
+            if 0 <= r < STEPS:
+                add_bias_and_mask(r)
+            if 0 <= r + QUANTISE_AHEAD < BLOCKS:
+                quantise_block(r + QUANTISE_AHEAD)
+            if 0 <= r < STEPS:
+                add_residual(r)
+                if r % STEPS_PER_GROUP == STEPS_PER_GROUP - 1:
+                    early_statistics(r // STEPS_PER_GROUP)
+            if 0 <= r - NORM_BEHIND < STEPS:
+                normalise_and_store(r - NORM_BEHIND)
+            if (r + RESIDUAL_AHEAD) % STEPS_PER_GROUP == 0 and 0 <= (r + RESIDUAL_AHEAD) // STEPS_PER_GROUP < GROUPS:
+                load_residual((r + RESIDUAL_AHEAD) // STEPS_PER_GROUP)

@@ -20,34 +20,32 @@ FLOPS = 2 * SEQS * FRAMES * C_IN * C_OUT
 WORDS = C_IN // 2
 BLOCK = 512
 ROWS = BLOCK // P
-BLOCKS_PER_SEQ = FRAMES // BLOCK
-BLOCKS = SEQS * BLOCKS_PER_SEQ
-STEP = 2 * BLOCK
-STEPS_PER_GROUP = FRAMES // STEP
-GROUPS = SEQS * (C_OUT // P)
-STEPS = GROUPS * STEPS_PER_GROUP
-STEPS_PER_SEQ = STEPS // SEQS
+CHUNK = 2 * BLOCK
+CHUNKS_PER_SEQ = FRAMES // CHUNK
+CHUNKS = SEQS * CHUNKS_PER_SEQ
+HALVES = C_OUT // P
+NORM_PART = 2 * CHUNK
 
-LOAD_AHEAD = 16
-FLIP_AHEAD = 8
-QUANTISE_AHEAD = FLIP_AHEAD - 1
+LAG = 2
+LOAD_AHEAD = 6
+FLIP_AHEAD = 2
+SPREAD_AHEAD = 1
 MULTIPLY_AHEAD = 1
 SQUARES_BEHIND = 1
-NORM_BEHIND = STEPS_PER_GROUP + 1
-SPREAD_AHEAD = 6
-RESIDUAL_AHEAD = 9
+NORM_BEHIND = CHUNKS_PER_SEQ + 1
+RESIDUAL_AHEAD = 5
 
-NORM_VECTOR_COLS = STEP // 2
+NORM_VECTOR_COLS = 3 * NORM_PART // 8
 
 
 def tile_transformerencoderblock_pa_t_kernel(tc, h_attn, x, masks, Wo, bo, out):
     nc = tc.nc
     with ExitStack() as ctx:
         const = ctx.enter_context(tc.tile_pool(name="const", bufs=1))
-        frames_in = ctx.enter_context(tc.tile_pool(name="frames_in", bufs=LOAD_AHEAD - FLIP_AHEAD))
-        stage = ctx.enter_context(tc.tile_pool(name="stage", bufs=3))
-        per_seq = ctx.enter_context(tc.tile_pool(name="per_seq", bufs=2))
-        per_group = ctx.enter_context(tc.tile_pool(name="per_group", bufs=3))
+        blocks_in = ctx.enter_context(tc.tile_pool(name="blocks_in", bufs=2 * (LOAD_AHEAD - FLIP_AHEAD)))
+        stage = ctx.enter_context(tc.tile_pool(name="stage", bufs=4))
+        per_chunk = ctx.enter_context(tc.tile_pool(name="per_chunk", bufs=FLIP_AHEAD + LAG))
+        per_group = ctx.enter_context(tc.tile_pool(name="per_group", bufs=4))
         psum = ctx.enter_context(tc.psum_pool(name="psum", bufs=1))
         ctx.enter_context(tc.manual_schedule())
 
@@ -85,115 +83,113 @@ def tile_transformerencoderblock_pa_t_kernel(tc, h_attn, x, masks, Wo, bo, out):
             out=small_rows[0:mask_row_count, :], in_=masks.rearrange("n o (i r) -> (n o i) r", r=P)
         )
         nc.scalar.dma_start(
-            out=small_rows[mask_row_count : mask_row_count + C_OUT // P, :],
+            out=small_rows[mask_row_count : mask_row_count + HALVES, :],
             in_=bo.rearrange("(h r) -> h r", r=P),
         )
-        w_raw = const.tile([P, 2 * C_IN], BF16)
+        w_raw = const.tile([P, HALVES * C_IN], BF16)
         nc.scalar.dma_start(
-            out=w_raw[:].rearrange("p (h k) -> p h k", h=2), in_=Wo.rearrange("(h p) k -> p h k", p=P)
+            out=w_raw[:].rearrange("p (h k) -> p h k", h=HALVES),
+            in_=Wo.rearrange("(h p) k -> p h k", p=P),
         )
+        mask_cols = const.tile([P, mask_row_count], BF16)
+        bias_cols = const.tile([P, HALVES], F32)
+        w_grouped = const.tile([P, HALVES * C_IN], BF16, align_bytes=64)
+        w_codes = const.tile([P, C_OUT], U32, align_bytes=64)
+        w_scales = const.tile([P, C_OUT], U8, align_bytes=64)
 
         def prepare_small_inputs():
-            small_cols = psum.tile([P, BLOCK], BF16, tag="spread", bufs=1)
+            small_cols = psum.tile([P, CHUNK], BF16, tag="spread", bufs=1)
             nc.tensor.transpose(small_cols[:, 0:P], small_rows[:], ident_bf16[:])
             nc.vector.tensor_copy(out=mask_cols[:], in_=small_cols[:, 0:mask_row_count])
             nc.vector.tensor_copy(
-                out=bias_cols[:], in_=small_cols[:, mask_row_count : mask_row_count + C_OUT // P]
+                out=bias_cols[:], in_=small_cols[:, mask_row_count : mask_row_count + HALVES]
             )
             flip_two(w_raw[:].bitcast(F32), w_grouped[:].bitcast(F32), True)
             nc.vector.quantize_mx(out=w_codes[:].bitcast(FP8X4), scales=w_scales[:], in_=w_grouped[:])
 
-        mask_cols = const.tile([P, mask_row_count], BF16)
-        bias_cols = const.tile([P, C_OUT // P], F32)
-        w_grouped = const.tile([P, 2 * C_IN], BF16, align_bytes=64)
-        w_codes = const.tile([P, C_OUT], U32, align_bytes=64)
-        w_scales = const.tile([P, C_OUT], U8, align_bytes=64)
+        def load_chunk(chunk):
+            seq, j = divmod(chunk, CHUNKS_PER_SEQ)
+            for i in range(CHUNK // BLOCK):
+                first = CHUNK * j + BLOCK * i
+                raw[(chunk, i)] = blocks_in.tile([P, ROWS * C_IN], BF16, name="raw")
+                nc.sync.dma_start(
+                    out=raw[(chunk, i)][:],
+                    in_=h_attn[seq, first : first + BLOCK, :].rearrange("(p a) k -> p (a k)", a=ROWS),
+                )
 
-        def load_block(block):
-            seq, b = divmod(block, BLOCKS_PER_SEQ)
-            raw[block] = frames_in.tile([P, ROWS * C_IN], BF16, name="raw")
-            nc.sync.dma_start(
-                out=raw[block][:],
-                in_=h_attn[seq, BLOCK * b : BLOCK * (b + 1), :].rearrange("(p a) k -> p (a k)", a=ROWS),
-            )
-
-        def load_residual(group):
-            seq, half = divmod(group, C_OUT // P)
+        def load_residual(seq, half):
+            group = (seq, half)
             residual[group] = per_group.tile([P, FRAMES], BF16, name="residual")
             nc.sync.dma_start(out=residual[group][:], in_=x[seq, P * half : P * (half + 1), :])
 
-        def flip_block(block):
-            seq, b = divmod(block, BLOCKS_PER_SEQ)
-            if b == 0:
-                codes[seq] = per_seq.tile([P, FRAMES], U32, name="codes", align_bytes=64)
-                scales[seq] = per_seq.tile([P, FRAMES], U8, name="scales", align_bytes=64)
-            grouped[block] = stage.tile([P, 4 * BLOCK], BF16, name="grouped", align_bytes=64)
-            raw_words = raw[block][:].bitcast(F32)
-            grouped_words = grouped[block][:].bitcast(F32)
-            for pair in range(ROWS // 2):
-                cols = slice(2 * WORDS * pair, 2 * WORDS * (pair + 1))
-                flip_two(raw_words[:, cols], grouped_words[:, cols], seq == 0 and pair == 1)
+        def flip_chunk(chunk, vector_helps):
+            for i in range(CHUNK // BLOCK):
+                grouped[(chunk, i)] = stage.tile([P, 4 * BLOCK], BF16, name="grouped", align_bytes=64)
+                raw_words = raw[(chunk, i)][:].bitcast(F32)
+                grouped_words = grouped[(chunk, i)][:].bitcast(F32)
+                for pair in range(ROWS // 2):
+                    cols = slice(2 * WORDS * pair, 2 * WORDS * (pair + 1))
+                    flip_two(raw_words[:, cols], grouped_words[:, cols], vector_helps and pair == 1)
 
-        def spread_mask(block):
-            seq, b = divmod(block, BLOCKS_PER_SEQ)
-            if b == 0:
-                mask_rows[seq] = per_seq.tile([P, FRAMES], BF16, name="mask_rows")
-            spread = psum.tile([P, BLOCK], BF16, tag="spread", bufs=1)
-            for i in range(BLOCK // P):
-                col = (FRAMES // P) * seq + (BLOCK // P) * b + i
+        def spread_mask(chunk):
+            mask_rows[chunk] = per_chunk.tile([P, CHUNK], BF16, name="mask_rows")
+            spread = psum.tile([P, CHUNK], BF16, tag="spread", bufs=1)
+            for i in range(CHUNK // P):
+                col = (CHUNK // P) * chunk + i
                 nc.tensor.transpose(
                     spread[:, P * i : P * (i + 1)],
                     mask_cols[:, col : col + 1].to_broadcast([P, P]),
                     ident_bf16[:],
                 )
-            nc.scalar.copy(out=mask_rows[seq][:, BLOCK * b : BLOCK * (b + 1)], in_=spread[:])
+            nc.scalar.copy(out=mask_rows[chunk][:], in_=spread[:])
 
-        def quantise_block(block):
-            seq, b = divmod(block, BLOCKS_PER_SEQ)
-            cols = slice(BLOCK * b, BLOCK * (b + 1))
+        def quantise_block(chunk, i):
+            if i == 0:
+                codes[chunk] = per_chunk.tile([P, CHUNK], U32, name="codes", align_bytes=64)
+                scales[chunk] = per_chunk.tile([P, CHUNK], U8, name="scales", align_bytes=64)
+            cols = slice(BLOCK * i, BLOCK * (i + 1))
             nc.vector.quantize_mx(
-                out=codes[seq][:, cols].bitcast(FP8X4), scales=scales[seq][:, cols], in_=grouped[block][:]
+                out=codes[chunk][:, cols].bitcast(FP8X4),
+                scales=scales[chunk][:, cols],
+                in_=grouped[(chunk, i)][:],
             )
 
-        def where(step):
-            group, j = divmod(step, STEPS_PER_GROUP)
-            seq, half = divmod(group, C_OUT // P)
-            return seq, half, group, j
-
-        def multiply(step):
-            seq, half, group, j = where(step)
-            for i in range(STEP // BLOCK):
-                cols = slice(STEP * j + BLOCK * i, STEP * j + BLOCK * (i + 1))
-                product[(step, i)] = psum.tile([P, BLOCK], F32, tag="product", bufs=4, name="product")
+        def multiply(chunk, half):
+            for i in range(CHUNK // BLOCK):
+                cols = slice(BLOCK * i, BLOCK * (i + 1))
+                product[(chunk, half, i)] = psum.tile([P, BLOCK], F32, tag="product", bufs=4, name="product")
                 nc.tensor.matmul_mx(
-                    out=product[(step, i)][:],
+                    out=product[(chunk, half, i)][:],
                     lhsT=w_codes[:, P * half : P * (half + 1)].bitcast(FP8X4),
                     lhsT_scale=w_scales[:, P * half : P * (half + 1)],
-                    rhs=codes[seq][:, cols].bitcast(FP8X4),
-                    rhs_scale=scales[seq][:, cols],
+                    rhs=codes[chunk][:, cols].bitcast(FP8X4),
+                    rhs_scale=scales[chunk][:, cols],
                     start=True,
                     stop=True,
                 )
 
-        def add_bias_and_mask(step):
-            seq, half, group, j = where(step)
+        def add_bias_and_mask(chunk, half):
+            seq, j = divmod(chunk, CHUNKS_PER_SEQ)
+            group = (seq, half)
             if j == 0:
                 y[group] = per_group.tile([P, FRAMES], F32, name="y")
                 sums[group] = per_group.tile([P, 2, 8], F32, name="sums")
-            for i in range(STEP // BLOCK):
-                cols = slice(STEP * j + BLOCK * i, STEP * j + BLOCK * (i + 1))
+            for i in range(CHUNK // BLOCK):
+                cols = slice(BLOCK * i, BLOCK * (i + 1))
+                first = CHUNK * j + BLOCK * i
                 nc.vector.scalar_tensor_tensor(
-                    out=y[group][:, cols].rearrange("e (p a) -> e p a", a=ROWS),
-                    in0=product[(step, i)][:].rearrange("e (a p) -> e p a", a=ROWS),
+                    out=y[group][:, first : first + BLOCK].rearrange("e (p a) -> e p a", a=ROWS),
+                    in0=product[(chunk, half, i)][:].rearrange("e (a p) -> e p a", a=ROWS),
                     scalar=bias_cols[:, half : half + 1],
-                    in1=mask_rows[seq][:, cols].rearrange("e (p a) -> e p a", a=ROWS),
+                    in1=mask_rows[chunk][:, cols].rearrange("e (p a) -> e p a", a=ROWS),
                     op0=ALU.add,
                     op1=ALU.mult,
                 )
 
-        def add_residual(step):
-            seq, half, group, j = where(step)
-            cols = slice(STEP * j, STEP * (j + 1))
+        def add_residual(chunk, half):
+            seq, j = divmod(chunk, CHUNKS_PER_SEQ)
+            group = (seq, half)
+            cols = slice(CHUNK * j, CHUNK * (j + 1))
             nc.vector.scalar_tensor_tensor(
                 out=y[group][:, cols],
                 in0=y[group][:, cols],
@@ -205,20 +201,24 @@ def tile_transformerencoderblock_pa_t_kernel(tc, h_attn, x, masks, Wo, bo, out):
             )
             if j == 0:
                 pivot[group] = per_group.tile([P, 2], F32, name="pivot")
-                for col, factor in enumerate((-1.0 / STEP, -ROOT_SCALE / STEP)):
+                for col, factor in enumerate((-1.0 / CHUNK, -ROOT_SCALE / CHUNK)):
                     nc.gpsimd.tensor_scalar(
                         out=pivot[group][:, col : col + 1], in0=sums[group][:, 0, 0:1],
                         scalar1=factor, scalar2=0.0, op0=ALU.mult, op1=ALU.add,
                     )
+            if j == CHUNKS_PER_SEQ - 1:
+                early_statistics(group)
 
-        def sum_squares(step):
-            seq, half, group, j = where(step)
-            cols = slice(STEP * j, STEP * (j + 1))
-            squares = stage.tile([P, STEP], BF16, name="squares")
+        def sum_squares(chunk, half):
+            seq, j = divmod(chunk, CHUNKS_PER_SEQ)
+            group = (seq, half)
+            squares = stage.tile([P, CHUNK], BF16, name="squares")
             nc.scalar.activation(
-                out=squares[:], in_=y[group][:, cols], func=ACT.Square,
+                out=squares[:], in_=y[group][:, CHUNK * j : CHUNK * (j + 1)], func=ACT.Square,
                 bias=pivot[group][:, 1:2], scale=ROOT_SCALE, accum_out=sums[group][:, 1, j : j + 1],
             )
+            if j == CHUNKS_PER_SEQ - 1:
+                late_statistics(group)
 
         def add_columns(total, row, count):
             nc.gpsimd.tensor_tensor(out=total, in0=row[:, 0:1], in1=row[:, 1:2], op=ALU.add)
@@ -227,14 +227,16 @@ def tile_transformerencoderblock_pa_t_kernel(tc, h_attn, x, masks, Wo, bo, out):
 
         def early_statistics(group):
             total = per_group.tile([P, 1], F32, name="total")
-            add_columns(total[:], sums[group][:, 0, :], STEPS_PER_GROUP)
+            add_columns(total[:], sums[group][:, 0, :], CHUNKS_PER_SEQ)
             neg_mean[group] = per_group.tile([P, 1], F32, name="neg_mean")
             nc.gpsimd.tensor_scalar(
                 out=neg_mean[group][:], in0=total[:],
                 scalar1=-1.0 / FRAMES, scalar2=0.0, op0=ALU.mult, op1=ALU.add,
             )
             off = per_group.tile([P, 1], F32, name="off")
-            nc.gpsimd.tensor_tensor(out=off[:], in0=neg_mean[group][:], in1=pivot[group][:, 0:1], op=ALU.subtract)
+            nc.gpsimd.tensor_tensor(
+                out=off[:], in0=neg_mean[group][:], in1=pivot[group][:, 0:1], op=ALU.subtract
+            )
             off_sq = per_group.tile([P, 1], F32, name="off_sq")
             nc.gpsimd.tensor_tensor(out=off_sq[:], in0=off[:], in1=off[:], op=ALU.mult)
             rest = per_group.tile([P, 1], F32, name="rest")
@@ -242,7 +244,7 @@ def tile_transformerencoderblock_pa_t_kernel(tc, h_attn, x, masks, Wo, bo, out):
                 out=rest[:], in0=off_sq[:], scalar1=-1.0, scalar2=EPS, op0=ALU.mult, op1=ALU.add
             )
             first_squares = per_group.tile([P, 1], F32, name="first_squares")
-            add_columns(first_squares[:], sums[group][:, 1, :], STEPS_PER_GROUP - 1)
+            add_columns(first_squares[:], sums[group][:, 1, :], CHUNKS_PER_SEQ - 1)
             base[group] = per_group.tile([P, 1], F32, name="base")
             nc.gpsimd.tensor_tensor(out=base[group][:], in0=first_squares[:], in1=rest[:], op=ALU.add)
 
@@ -250,16 +252,19 @@ def tile_transformerencoderblock_pa_t_kernel(tc, h_attn, x, masks, Wo, bo, out):
             var_eps = per_group.tile([P, 1], F32, name="var_eps")
             nc.gpsimd.tensor_tensor(
                 out=var_eps[:], in0=base[group][:],
-                in1=sums[group][:, 1, STEPS_PER_GROUP - 1 : STEPS_PER_GROUP], op=ALU.add,
+                in1=sums[group][:, 1, CHUNKS_PER_SEQ - 1 : CHUNKS_PER_SEQ], op=ALU.add,
             )
             rstd[group] = per_group.tile([P, 1], F32, name="rstd")
             nc.gpsimd.tensor_tensor(out=rstd[group][:], in0=var_eps[:], in1=minus_half[:], op=ALU.pow)
             shift[group] = per_group.tile([P, 1], F32, name="shift")
-            nc.gpsimd.tensor_tensor(out=shift[group][:], in0=neg_mean[group][:], in1=rstd[group][:], op=ALU.mult)
+            nc.gpsimd.tensor_tensor(
+                out=shift[group][:], in0=neg_mean[group][:], in1=rstd[group][:], op=ALU.mult
+            )
 
-        def normalise_and_store(step):
-            seq, half, group, j = where(step)
-            first, split, last = STEP * j, STEP * j + NORM_VECTOR_COLS, STEP * (j + 1)
+        def normalise_and_store(seq, half, part):
+            group = (seq, half)
+            first, last = NORM_PART * part, NORM_PART * (part + 1)
+            split = first + NORM_VECTOR_COLS
             nc.vector.tensor_scalar(
                 out=y[group][:, first:split], in0=y[group][:, first:split],
                 scalar1=rstd[group][:, 0:1], scalar2=shift[group][:, 0:1], op0=ALU.mult, op1=ALU.add,
@@ -268,32 +273,41 @@ def tile_transformerencoderblock_pa_t_kernel(tc, h_attn, x, masks, Wo, bo, out):
                 out=y[group][:, split:last], in_=y[group][:, split:last], func=ACT.Identity,
                 bias=shift[group][:, 0:1], scale=rstd[group][:, 0:1],
             )
-            nc.sync.dma_start(out=out[seq, P * half : P * (half + 1), first:last], in_=y[group][:, first:last])
+            nc.sync.dma_start(
+                out=out[seq, P * half : P * (half + 1), first:last], in_=y[group][:, first:last]
+            )
 
-        for r in range(-LOAD_AHEAD, STEPS + NORM_BEHIND):
-            if 0 <= r + MULTIPLY_AHEAD < STEPS:
-                multiply(r + MULTIPLY_AHEAD)
-            if 0 <= r + FLIP_AHEAD < BLOCKS:
-                flip_block(r + FLIP_AHEAD)
+        def live(chunk):
+            return 0 <= chunk < CHUNKS
+
+        for r in range(-LOAD_AHEAD, CHUNKS + LAG + NORM_BEHIND - CHUNKS_PER_SEQ + FRAMES // NORM_PART):
+            if live(r + FLIP_AHEAD):
+                flip_chunk(r + FLIP_AHEAD, r < 0)
             if r == -SPREAD_AHEAD:
                 prepare_small_inputs()
-            if 0 <= r + SPREAD_AHEAD < BLOCKS:
+            if live(r + SPREAD_AHEAD):
                 spread_mask(r + SPREAD_AHEAD)
-            if 0 <= r + LOAD_AHEAD < BLOCKS:
-                load_block(r + LOAD_AHEAD)
-            if 0 <= r - SQUARES_BEHIND < STEPS:
-                sum_squares(r - SQUARES_BEHIND)
-                if (r - SQUARES_BEHIND) % STEPS_PER_GROUP == STEPS_PER_GROUP - 1:
-                    late_statistics((r - SQUARES_BEHIND) // STEPS_PER_GROUP)
-            if 0 <= r < STEPS:
-                add_bias_and_mask(r)
-            if 0 <= r + QUANTISE_AHEAD < BLOCKS:
-                quantise_block(r + QUANTISE_AHEAD)
-            if 0 <= r < STEPS:
-                add_residual(r)
-                if r % STEPS_PER_GROUP == STEPS_PER_GROUP - 1:
-                    early_statistics(r // STEPS_PER_GROUP)
-            if 0 <= r - NORM_BEHIND < STEPS:
-                normalise_and_store(r - NORM_BEHIND)
-            if (r + RESIDUAL_AHEAD) % STEPS_PER_GROUP == 0 and 0 <= (r + RESIDUAL_AHEAD) // STEPS_PER_GROUP < GROUPS:
-                load_residual((r + RESIDUAL_AHEAD) // STEPS_PER_GROUP)
+            if live(r + LOAD_AHEAD):
+                load_chunk(r + LOAD_AHEAD)
+            for half in range(HALVES):
+                if live(r - LAG * half):
+                    add_bias_and_mask(r - LAG * half, half)
+            for half in range(HALVES):
+                if live(r - LAG * half + MULTIPLY_AHEAD):
+                    multiply(r - LAG * half + MULTIPLY_AHEAD, half)
+            for half in range(HALVES):
+                if live(r - LAG * half - SQUARES_BEHIND):
+                    sum_squares(r - LAG * half - SQUARES_BEHIND, half)
+            for half in range(HALVES):
+                if live(r + FLIP_AHEAD):
+                    quantise_block(r + FLIP_AHEAD, half)
+                if live(r - LAG * half):
+                    add_residual(r - LAG * half, half)
+            for half in range(HALVES):
+                seq, part = divmod(r - LAG * half - NORM_BEHIND, CHUNKS_PER_SEQ)
+                if 0 <= seq < SEQS and part < FRAMES // NORM_PART:
+                    normalise_and_store(seq, half, part)
+            for half in range(HALVES):
+                seq, j = divmod(r - LAG * half + RESIDUAL_AHEAD, CHUNKS_PER_SEQ)
+                if 0 <= seq < SEQS and j == 0:
+                    load_residual(seq, half)

@@ -35,7 +35,7 @@ SQUARES_BEHIND = 1
 NORM_BEHIND = CHUNKS_PER_SEQ + 1
 RESIDUAL_AHEAD = 5
 
-NORM_VECTOR_COLS = 3 * NORM_PART // 8
+NORM_SCALAR_COLS = 3 * NORM_PART // 8
 
 
 def tile_transformerencoderblock_pa_t_kernel(tc, h_attn, x, masks, Wo, bo, out):
@@ -264,14 +264,14 @@ def tile_transformerencoderblock_pa_t_kernel(tc, h_attn, x, masks, Wo, bo, out):
         def normalise_and_store(seq, half, part):
             group = (seq, half)
             first, last = NORM_PART * part, NORM_PART * (part + 1)
-            split = first + NORM_VECTOR_COLS
-            nc.vector.tensor_scalar(
-                out=y[group][:, first:split], in0=y[group][:, first:split],
-                scalar1=rstd[group][:, 0:1], scalar2=shift[group][:, 0:1], op0=ALU.mult, op1=ALU.add,
-            )
+            split = first + NORM_SCALAR_COLS
             nc.scalar.activation(
-                out=y[group][:, split:last], in_=y[group][:, split:last], func=ACT.Identity,
+                out=y[group][:, first:split], in_=y[group][:, first:split], func=ACT.Identity,
                 bias=shift[group][:, 0:1], scale=rstd[group][:, 0:1],
+            )
+            nc.gpsimd.tensor_scalar(
+                out=y[group][:, split:last], in0=y[group][:, split:last],
+                scalar1=rstd[group][:, 0:1], scalar2=shift[group][:, 0:1], op0=ALU.mult, op1=ALU.add,
             )
             nc.sync.dma_start(
                 out=out[seq, P * half : P * (half + 1), first:last], in_=y[group][:, first:last]

@@ -35,7 +35,8 @@ SQUARES_BEHIND = 1
 NORM_BEHIND = CHUNKS_PER_SEQ + 1
 RESIDUAL_AHEAD = 5
 
-NORM_SCALAR_COLS = 3 * NORM_PART // 8
+NORM_VECTOR_COLS = 3 * NORM_PART // 8
+NORM_VECTOR_COLS_END = 21 * NORM_PART // 32
 
 
 def tile_transformerencoderblock_pa_t_kernel(tc, h_attn, x, masks, Wo, bo, out):
@@ -51,8 +52,6 @@ def tile_transformerencoderblock_pa_t_kernel(tc, h_attn, x, masks, Wo, bo, out):
 
         ident_f32 = const.tile([P, P], F32)
         make_identity(nc, ident_f32[:])
-        ident_bf16 = const.tile([P, P], BF16)
-        make_identity(nc, ident_bf16[:])
         minus_half = const.tile([P, 1], F32)
         nc.gpsimd.memset(minus_half[:], -0.5)
 
@@ -76,36 +75,35 @@ def tile_transformerencoderblock_pa_t_kernel(tc, h_attn, x, masks, Wo, bo, out):
             else:
                 nc.scalar.copy(out=dst, in_=src)
 
-        small_rows = const.tile([P, P], BF16)
+        small_rows = const.tile([P, 2 * P], BF16)
         nc.vector.memset(small_rows[:], 0.0)
-        mask_row_count = SEQS * FRAMES // P
+        mask_row_count = SEQS * FRAMES // (2 * P)
         nc.scalar.dma_start(
-            out=small_rows[0:mask_row_count, :], in_=masks.rearrange("n o (i r) -> (n o i) r", r=P)
+            out=small_rows[0:mask_row_count, :], in_=masks.rearrange("n o (i r) -> (n o i) r", r=2 * P)
         )
         nc.scalar.dma_start(
-            out=small_rows[mask_row_count : mask_row_count + HALVES, :],
-            in_=bo.rearrange("(h r) -> h r", r=P),
+            out=small_rows[mask_row_count : mask_row_count + 1, :], in_=bo.rearrange("(o c) -> o c", o=1)
         )
         w_raw = const.tile([P, HALVES * C_IN], BF16)
-        nc.scalar.dma_start(
-            out=w_raw[:].rearrange("p (h k) -> p h k", h=HALVES),
-            in_=Wo.rearrange("(h p) k -> p h k", p=P),
-        )
-        mask_cols = const.tile([P, mask_row_count], BF16)
+        nc.scalar.dma_start(out=w_raw[:], in_=Wo.rearrange("(p h) k -> p (h k)", h=HALVES))
+        mask_words = const.tile([P, mask_row_count], F32)
         bias_cols = const.tile([P, HALVES], F32)
         w_grouped = const.tile([P, HALVES * C_IN], BF16, align_bytes=64)
         w_codes = const.tile([P, C_OUT], U32, align_bytes=64)
         w_scales = const.tile([P, C_OUT], U8, align_bytes=64)
 
         def prepare_small_inputs():
-            small_cols = psum.tile([P, CHUNK], BF16, tag="spread", bufs=1)
-            nc.tensor.transpose(small_cols[:, 0:P], small_rows[:], ident_bf16[:])
-            nc.vector.tensor_copy(out=mask_cols[:], in_=small_cols[:, 0:mask_row_count])
+            small_cols = psum.tile([P, CHUNK // 2], F32, tag="spread", bufs=1)
+            nc.tensor.transpose(small_cols[:, 0:P], small_rows[:].bitcast(F32), ident_f32[:])
+            nc.vector.tensor_copy(out=mask_words[:], in_=small_cols[:, 0:mask_row_count])
             nc.vector.tensor_copy(
-                out=bias_cols[:], in_=small_cols[:, mask_row_count : mask_row_count + HALVES]
+                out=bias_cols[:], in_=small_cols[:, mask_row_count : mask_row_count + 1].bitcast(BF16)
             )
             flip_two(w_raw[:].bitcast(F32), w_grouped[:].bitcast(F32), True)
             nc.vector.quantize_mx(out=w_codes[:].bitcast(FP8X4), scales=w_scales[:], in_=w_grouped[:])
+
+        x_halves = x.rearrange("n (p h) t -> n h p t", h=HALVES)
+        out_halves = out.rearrange("n (p h) t -> n h p t", h=HALVES)
 
         def load_chunk(chunk):
             seq, j = divmod(chunk, CHUNKS_PER_SEQ)
@@ -120,7 +118,7 @@ def tile_transformerencoderblock_pa_t_kernel(tc, h_attn, x, masks, Wo, bo, out):
         def load_residual(seq, half):
             group = (seq, half)
             residual[group] = per_group.tile([P, FRAMES], BF16, name="residual")
-            nc.sync.dma_start(out=residual[group][:], in_=x[seq, P * half : P * (half + 1), :])
+            nc.sync.dma_start(out=residual[group][:], in_=x_halves[seq, half])
 
         def flip_chunk(chunk, vector_helps):
             for i in range(CHUNK // BLOCK):
@@ -133,15 +131,15 @@ def tile_transformerencoderblock_pa_t_kernel(tc, h_attn, x, masks, Wo, bo, out):
 
         def spread_mask(chunk):
             mask_rows[chunk] = per_chunk.tile([P, CHUNK], BF16, name="mask_rows")
-            spread = psum.tile([P, CHUNK], BF16, tag="spread", bufs=1)
-            for i in range(CHUNK // P):
-                col = (CHUNK // P) * chunk + i
+            spread = psum.tile([P, CHUNK // 2], F32, tag="spread", bufs=1)
+            for i in range(CHUNK // (2 * P)):
+                col = CHUNK // (2 * P) * chunk + i
                 nc.tensor.transpose(
                     spread[:, P * i : P * (i + 1)],
-                    mask_cols[:, col : col + 1].to_broadcast([P, P]),
-                    ident_bf16[:],
+                    mask_words[:, col : col + 1].to_broadcast([P, P]),
+                    ident_f32[:],
                 )
-            nc.scalar.copy(out=mask_rows[chunk][:], in_=spread[:])
+            nc.scalar.copy(out=mask_rows[chunk][:], in_=spread[:].bitcast(BF16))
 
         def quantise_block(chunk, i):
             if i == 0:
@@ -261,20 +259,20 @@ def tile_transformerencoderblock_pa_t_kernel(tc, h_attn, x, masks, Wo, bo, out):
                 out=shift[group][:], in0=neg_mean[group][:], in1=rstd[group][:], op=ALU.mult
             )
 
-        def normalise_and_store(seq, half, part):
+        def normalise_and_store(seq, half, part, vector_cols):
             group = (seq, half)
             first, last = NORM_PART * part, NORM_PART * (part + 1)
-            split = first + NORM_SCALAR_COLS
-            nc.scalar.activation(
-                out=y[group][:, first:split], in_=y[group][:, first:split], func=ACT.Identity,
-                bias=shift[group][:, 0:1], scale=rstd[group][:, 0:1],
-            )
-            nc.gpsimd.tensor_scalar(
-                out=y[group][:, split:last], in0=y[group][:, split:last],
+            split = first + vector_cols
+            nc.vector.tensor_scalar(
+                out=y[group][:, first:split], in0=y[group][:, first:split],
                 scalar1=rstd[group][:, 0:1], scalar2=shift[group][:, 0:1], op0=ALU.mult, op1=ALU.add,
             )
+            nc.scalar.activation(
+                out=y[group][:, split:last], in_=y[group][:, split:last], func=ACT.Identity,
+                bias=shift[group][:, 0:1], scale=rstd[group][:, 0:1],
+            )
             nc.sync.dma_start(
-                out=out[seq, P * half : P * (half + 1), first:last], in_=y[group][:, first:last]
+                out=out_halves[seq, half, :, first:last], in_=y[group][:, first:last]
             )
 
         def live(chunk):
@@ -306,7 +304,8 @@ def tile_transformerencoderblock_pa_t_kernel(tc, h_attn, x, masks, Wo, bo, out):
             for half in range(HALVES):
                 seq, part = divmod(r - LAG * half - NORM_BEHIND, CHUNKS_PER_SEQ)
                 if 0 <= seq < SEQS and part < FRAMES // NORM_PART:
-                    normalise_and_store(seq, half, part)
+                    busy = r < CHUNKS + LAG
+                    normalise_and_store(seq, half, part, NORM_VECTOR_COLS if busy else NORM_VECTOR_COLS_END)
             for half in range(HALVES):
                 seq, j = divmod(r - LAG * half + RESIDUAL_AHEAD, CHUNKS_PER_SEQ)
                 if 0 <= seq < SEQS and j == 0:

from contextlib import ExitStack

import concourse.mybir as mybir
from concourse.masks import make_identity

F32 = mybir.dt.float32
BF16 = mybir.dt.bfloat16
U32 = mybir.dt.uint32
U8 = mybir.dt.uint8
FP8X4 = mybir.dt.float8_e4m3fn_x4
ALU = mybir.AluOpType
ACT = mybir.ActivationFunctionType

P = 128
SEQS, FRAMES, C_IN, C_OUT = 3, 4096, 512, 256
EPS = 1e-5
ROOT_SCALE = FRAMES**-0.5
FLOPS = 2 * SEQS * FRAMES * C_IN * C_OUT

WORDS = C_IN // 2
BLOCK = 512
ROWS = BLOCK // P
CHUNK = 2 * BLOCK
CHUNKS_PER_SEQ = FRAMES // CHUNK
CHUNKS = SEQS * CHUNKS_PER_SEQ
HALVES = C_OUT // P
NORM_PART = 2 * CHUNK

LAG = 2
LOAD_AHEAD = 6
FLIP_AHEAD = 2
SPREAD_AHEAD = 1
MULTIPLY_AHEAD = 1
SQUARES_BEHIND = 1
NORM_BEHIND = CHUNKS_PER_SEQ + 1
RESIDUAL_AHEAD = 5

NORM_VECTOR_COLS = 3 * NORM_PART // 8
NORM_VECTOR_COLS_END = 21 * NORM_PART // 32


def tile_transformerencoderblock_pa_t_kernel(tc, h_attn, x, masks, Wo, bo, out):
    nc = tc.nc
    with ExitStack() as ctx:
        const = ctx.enter_context(tc.tile_pool(name="const", bufs=1))
        blocks_in = ctx.enter_context(tc.tile_pool(name="blocks_in", bufs=2 * (LOAD_AHEAD - FLIP_AHEAD)))
        stage = ctx.enter_context(tc.tile_pool(name="stage", bufs=4))
        per_chunk = ctx.enter_context(tc.tile_pool(name="per_chunk", bufs=FLIP_AHEAD + LAG))
        per_group = ctx.enter_context(tc.tile_pool(name="per_group", bufs=4))
        psum = ctx.enter_context(tc.psum_pool(name="psum", bufs=1))
        ctx.enter_context(tc.manual_schedule())

        ident_f32 = const.tile([P, P], F32)
        make_identity(nc, ident_f32[:])
        minus_half = const.tile([P, 1], F32)
        nc.gpsimd.memset(minus_half[:], -0.5)

        raw, grouped = {}, {}
        codes, scales, mask_rows = {}, {}, {}
        product = {}
        residual, y, sums, pivot, neg_mean, base, rstd, shift = {}, {}, {}, {}, {}, {}, {}, {}

        def flip_two(rows_words, grouped_words, by_vector):
            bank = psum.tile([P, 2, 2, P], F32, tag="flip", bufs=3)
            for row_block in range(2):
                for half_row in range(2):
                    first = WORDS * row_block + P * half_row
                    nc.tensor.transpose(
                        bank[:, row_block, half_row, :], rows_words[:, first : first + P], ident_f32[:]
                    )
            dst = grouped_words.rearrange("w (b r u) -> w b r u", b=2, u=2)
            src = bank[:].rearrange("w b u r -> w b r u")
            if by_vector:
                nc.vector.tensor_copy(out=dst, in_=src)
            else:
                nc.scalar.copy(out=dst, in_=src)

        small_rows = const.tile([P, 2 * P], BF16)
        nc.vector.memset(small_rows[:], 0.0)
        mask_row_count = SEQS * FRAMES // (2 * P)
        nc.scalar.dma_start(
            out=small_rows[0:mask_row_count, :], in_=masks.rearrange("n o (i r) -> (n o i) r", r=2 * P)
        )
        nc.scalar.dma_start(
            out=small_rows[mask_row_count : mask_row_count + 1, :], in_=bo.rearrange("(o c) -> o c", o=1)
        )
        w_raw = const.tile([P, HALVES * C_IN], BF16)
        nc.scalar.dma_start(out=w_raw[:], in_=Wo.rearrange("(p h) k -> p (h k)", h=HALVES))
        mask_words = const.tile([P, mask_row_count], F32)
        bias_cols = const.tile([P, HALVES], F32)
        w_grouped = const.tile([P, HALVES * C_IN], BF16, align_bytes=64)
        w_codes = const.tile([P, C_OUT], U32, align_bytes=64)
        w_scales = const.tile([P, C_OUT], U8, align_bytes=64)

        def prepare_small_inputs():
            small_cols = psum.tile([P, CHUNK // 2], F32, tag="spread", bufs=1)
            nc.tensor.transpose(small_cols[:, 0:P], small_rows[:].bitcast(F32), ident_f32[:])
            nc.vector.tensor_copy(out=mask_words[:], in_=small_cols[:, 0:mask_row_count])
            nc.vector.tensor_copy(
                out=bias_cols[:], in_=small_cols[:, mask_row_count : mask_row_count + 1].bitcast(BF16)
            )
            flip_two(w_raw[:].bitcast(F32), w_grouped[:].bitcast(F32), True)
            nc.vector.quantize_mx(out=w_codes[:].bitcast(FP8X4), scales=w_scales[:], in_=w_grouped[:])

        x_halves = x.rearrange("n (p h) t -> n h p t", h=HALVES)
        out_halves = out.rearrange("n (p h) t -> n h p t", h=HALVES)

        def load_chunk(chunk):
            seq, j = divmod(chunk, CHUNKS_PER_SEQ)
            for i in range(CHUNK // BLOCK):
                first = CHUNK * j + BLOCK * i
                raw[(chunk, i)] = blocks_in.tile([P, ROWS * C_IN], BF16, name="raw")
                nc.sync.dma_start(
                    out=raw[(chunk, i)][:],
                    in_=h_attn[seq, first : first + BLOCK, :].rearrange("(p a) k -> p (a k)", a=ROWS),
                )

        def load_residual(seq, half):
            group = (seq, half)
            residual[group] = per_group.tile([P, FRAMES], BF16, name="residual")
            nc.sync.dma_start(out=residual[group][:], in_=x_halves[seq, half])

        def flip_chunk(chunk, vector_helps):
            for i in range(CHUNK // BLOCK):
                grouped[(chunk, i)] = stage.tile([P, 4 * BLOCK], BF16, name="grouped", align_bytes=64)
                raw_words = raw[(chunk, i)][:].bitcast(F32)
                grouped_words = grouped[(chunk, i)][:].bitcast(F32)
                for pair in range(ROWS // 2):
                    cols = slice(2 * WORDS * pair, 2 * WORDS * (pair + 1))
                    flip_two(raw_words[:, cols], grouped_words[:, cols], vector_helps and pair == 1)

        def spread_mask(chunk):
            mask_rows[chunk] = per_chunk.tile([P, CHUNK], BF16, name="mask_rows")
            spread = psum.tile([P, CHUNK // 2], F32, tag="spread", bufs=1)
            for i in range(CHUNK // (2 * P)):
                col = CHUNK // (2 * P) * chunk + i
                nc.tensor.transpose(
                    spread[:, P * i : P * (i + 1)],
                    mask_words[:, col : col + 1].to_broadcast([P, P]),
                    ident_f32[:],
                )
            nc.scalar.copy(out=mask_rows[chunk][:], in_=spread[:].bitcast(BF16))

        def quantise_block(chunk, i):
            if i == 0:
                codes[chunk] = per_chunk.tile([P, CHUNK], U32, name="codes", align_bytes=64)
                scales[chunk] = per_chunk.tile([P, CHUNK], U8, name="scales", align_bytes=64)
            cols = slice(BLOCK * i, BLOCK * (i + 1))
            nc.vector.quantize_mx(
                out=codes[chunk][:, cols].bitcast(FP8X4),
                scales=scales[chunk][:, cols],
                in_=grouped[(chunk, i)][:],
            )

        def multiply(chunk, half):
            for i in range(CHUNK // BLOCK):
                cols = slice(BLOCK * i, BLOCK * (i + 1))
                product[(chunk, half, i)] = psum.tile([P, BLOCK], F32, tag="product", bufs=4, name="product")
                nc.tensor.matmul_mx(
                    out=product[(chunk, half, i)][:],
                    lhsT=w_codes[:, P * half : P * (half + 1)].bitcast(FP8X4),
                    lhsT_scale=w_scales[:, P * half : P * (half + 1)],
                    rhs=codes[chunk][:, cols].bitcast(FP8X4),
                    rhs_scale=scales[chunk][:, cols],
                    start=True,
                    stop=True,
                )

        def add_bias_and_mask(chunk, half):
            seq, j = divmod(chunk, CHUNKS_PER_SEQ)
            group = (seq, half)
            if j == 0:
                y[group] = per_group.tile([P, FRAMES], F32, name="y")
                sums[group] = per_group.tile([P, 2, 8], F32, name="sums")
            for i in range(CHUNK // BLOCK):
                cols = slice(BLOCK * i, BLOCK * (i + 1))
                first = CHUNK * j + BLOCK * i
                nc.vector.scalar_tensor_tensor(
                    out=y[group][:, first : first + BLOCK].rearrange("e (p a) -> e p a", a=ROWS),
                    in0=product[(chunk, half, i)][:].rearrange("e (a p) -> e p a", a=ROWS),
                    scalar=bias_cols[:, half : half + 1],
                    in1=mask_rows[chunk][:, cols].rearrange("e (p a) -> e p a", a=ROWS),
                    op0=ALU.add,
                    op1=ALU.mult,
                )

        def add_residual(chunk, half):
            seq, j = divmod(chunk, CHUNKS_PER_SEQ)
            group = (seq, half)
            cols = slice(CHUNK * j, CHUNK * (j + 1))
            nc.vector.scalar_tensor_tensor(
                out=y[group][:, cols],
                in0=y[group][:, cols],
                scalar=1.0,
                in1=residual[group][:, cols],
                op0=ALU.mult,
                op1=ALU.add,
                accum_out=sums[group][:, 0, j : j + 1],
            )
            if j == 0:
                pivot[group] = per_group.tile([P, 2], F32, name="pivot")
                for col, factor in enumerate((-1.0 / CHUNK, -ROOT_SCALE / CHUNK)):
                    nc.gpsimd.tensor_scalar(
                        out=pivot[group][:, col : col + 1], in0=sums[group][:, 0, 0:1],
                        scalar1=factor, scalar2=0.0, op0=ALU.mult, op1=ALU.add,
                    )
            if j == CHUNKS_PER_SEQ - 1:
                early_statistics(group)

        def sum_squares(chunk, half):
            seq, j = divmod(chunk, CHUNKS_PER_SEQ)
            group = (seq, half)
            squares = stage.tile([P, CHUNK], BF16, name="squares")
            nc.scalar.activation(
                out=squares[:], in_=y[group][:, CHUNK * j : CHUNK * (j + 1)], func=ACT.Square,
                bias=pivot[group][:, 1:2], scale=ROOT_SCALE, accum_out=sums[group][:, 1, j : j + 1],
            )
            if j == CHUNKS_PER_SEQ - 1:
                late_statistics(group)

        def add_columns(total, row, count):
            nc.gpsimd.tensor_tensor(out=total, in0=row[:, 0:1], in1=row[:, 1:2], op=ALU.add)
            for col in range(2, count):
                nc.gpsimd.tensor_tensor(out=total, in0=total, in1=row[:, col : col + 1], op=ALU.add)

        def early_statistics(group):
            total = per_group.tile([P, 1], F32, name="total")
            add_columns(total[:], sums[group][:, 0, :], CHUNKS_PER_SEQ)
            neg_mean[group] = per_group.tile([P, 1], F32, name="neg_mean")
            nc.gpsimd.tensor_scalar(
                out=neg_mean[group][:], in0=total[:],
                scalar1=-1.0 / FRAMES, scalar2=0.0, op0=ALU.mult, op1=ALU.add,
            )
            off = per_group.tile([P, 1], F32, name="off")
            nc.gpsimd.tensor_tensor(
                out=off[:], in0=neg_mean[group][:], in1=pivot[group][:, 0:1], op=ALU.subtract
            )
            off_sq = per_group.tile([P, 1], F32, name="off_sq")
            nc.gpsimd.tensor_tensor(out=off_sq[:], in0=off[:], in1=off[:], op=ALU.mult)
            rest = per_group.tile([P, 1], F32, name="rest")
            nc.gpsimd.tensor_scalar(
                out=rest[:], in0=off_sq[:], scalar1=-1.0, scalar2=EPS, op0=ALU.mult, op1=ALU.add
            )
            first_squares = per_group.tile([P, 1], F32, name="first_squares")
            add_columns(first_squares[:], sums[group][:, 1, :], CHUNKS_PER_SEQ - 1)
            base[group] = per_group.tile([P, 1], F32, name="base")
            nc.gpsimd.tensor_tensor(out=base[group][:], in0=first_squares[:], in1=rest[:], op=ALU.add)

        def late_statistics(group):
            var_eps = per_group.tile([P, 1], F32, name="var_eps")
            nc.gpsimd.tensor_tensor(
                out=var_eps[:], in0=base[group][:],
                in1=sums[group][:, 1, CHUNKS_PER_SEQ - 1 : CHUNKS_PER_SEQ], op=ALU.add,
            )
            rstd[group] = per_group.tile([P, 1], F32, name="rstd")
            nc.gpsimd.tensor_tensor(out=rstd[group][:], in0=var_eps[:], in1=minus_half[:], op=ALU.pow)
            shift[group] = per_group.tile([P, 1], F32, name="shift")
            nc.gpsimd.tensor_tensor(
                out=shift[group][:], in0=neg_mean[group][:], in1=rstd[group][:], op=ALU.mult
            )

        def normalise_and_store(seq, half, part, vector_cols):
            group = (seq, half)
            first, last = NORM_PART * part, NORM_PART * (part + 1)
            split = first + vector_cols
            nc.vector.tensor_scalar(
                out=y[group][:, first:split], in0=y[group][:, first:split],
                scalar1=rstd[group][:, 0:1], scalar2=shift[group][:, 0:1], op0=ALU.mult, op1=ALU.add,
            )
            nc.scalar.activation(
                out=y[group][:, split:last], in_=y[group][:, split:last], func=ACT.Identity,
                bias=shift[group][:, 0:1], scale=rstd[group][:, 0:1],
            )
            nc.sync.dma_start(
                out=out_halves[seq, half, :, first:last], in_=y[group][:, first:last]
            )

        def live(chunk):
            return 0 <= chunk < CHUNKS

        for r in range(-LOAD_AHEAD, CHUNKS + LAG + NORM_BEHIND - CHUNKS_PER_SEQ + FRAMES // NORM_PART):
            if live(r + FLIP_AHEAD):
                flip_chunk(r + FLIP_AHEAD, r < 0)
            if r == -SPREAD_AHEAD:
                prepare_small_inputs()
            if live(r + SPREAD_AHEAD):
                spread_mask(r + SPREAD_AHEAD)
            if live(r + LOAD_AHEAD):
                load_chunk(r + LOAD_AHEAD)
            for half in range(HALVES):
                if live(r - LAG * half):
                    add_bias_and_mask(r - LAG * half, half)
            for half in range(HALVES):
                if live(r - LAG * half + MULTIPLY_AHEAD):
                    multiply(r - LAG * half + MULTIPLY_AHEAD, half)
            for half in range(HALVES):
                if live(r - LAG * half - SQUARES_BEHIND):
                    sum_squares(r - LAG * half - SQUARES_BEHIND, half)
            for half in range(HALVES):
                if live(r + FLIP_AHEAD):
                    quantise_block(r + FLIP_AHEAD, half)
                if live(r - LAG * half):
                    add_residual(r - LAG * half, half)
            for half in range(HALVES):
                seq, part = divmod(r - LAG * half - NORM_BEHIND, CHUNKS_PER_SEQ)
                if 0 <= seq < SEQS and part < FRAMES // NORM_PART:
                    busy = r < CHUNKS + LAG
                    normalise_and_store(seq, half, part, NORM_VECTOR_COLS if busy else NORM_VECTOR_COLS_END)
            for half in range(HALVES):
                seq, j = divmod(r - LAG * half + RESIDUAL_AHEAD, CHUNKS_PER_SEQ)
                if 0 <= seq < SEQS and j == 0:
                    load_residual(seq, half)
